import numpy as np
import ml_dtypes


def mxq(x, axis, fmt="e4m3"):
    dtype, down = {"e4m3": (ml_dtypes.float8_e4m3fn, 7), "e5m2": (ml_dtypes.float8_e5m2, 14)}[fmt]
    v = np.moveaxis(np.asarray(x, np.float32).astype(ml_dtypes.bfloat16).astype(np.float64), axis, -1)
    blocks = v.reshape(v.shape[:-1] + (-1, 32))
    amax = np.abs(blocks).max(-1, keepdims=True)
    byte = np.maximum(np.where(amax > 0, np.frexp(amax)[1] - 1 + 127, 0) - down, 1)
    scale = np.exp2(byte - 127.0)
    codes = (blocks / scale).astype(np.float32).astype(dtype).astype(np.float64)
    return np.moveaxis((codes * scale).reshape(v.shape), -1, axis)


WIDE = False


def mx_kscale(k):
    if not WIDE:
        return np.ones(k)
    levels = np.array([30, -30])
    if k % 512:
        return np.exp2(np.random.permutation(np.resize(levels, k // 32))).repeat(32)
    a = np.empty((k // 512, 16))
    for p in range(k // 512):
        a[p, :8] = np.random.permutation(np.resize(levels, 8))
        for g in range(8):
            far = levels[np.abs(levels - a[p, g]) >= 10]
            a[p, g + 8] = far[np.random.randint(len(far))]
    return np.exp2(a.ravel()).repeat(32)


BF16 = ml_dtypes.bfloat16


def bf(x):
    return np.asarray(x, np.float32).astype(BF16)


def f64(x):
    return np.asarray(x).astype(np.float64)


E2M1 = np.array([0.0, 0.5, 1.0, 1.5, 2.0, 3.0, 4.0, 6.0, -0.0, -0.5, -1.0, -1.5, -2.0, -3.0, -4.0, -6.0])


def pack_weight(w, fmt):
    k, n = w.shape
    w = f64(bf(w)).reshape(k // 32, 32, n)
    amax = np.abs(w).max(1)
    if fmt == "e4m3":
        byte = np.frexp(amax)[1] - 1 + 127 - 7
    else:
        mant, ex = np.frexp(amax / 6.0)
        byte = np.where(mant > 0.5, ex, ex - 1) + 127
    byte = np.clip(np.where(amax > 0, byte, 1), 1, 254)
    scaled = (w * np.exp2(127.0 - byte)[:, None, :]).reshape(k, n).astype(np.float32)
    by_word = np.ascontiguousarray(scaled.reshape(k // 512, 128, 4, n).transpose(0, 1, 3, 2))
    if fmt == "e4m3":
        words = by_word.astype(ml_dtypes.float8_e4m3fn).view(np.uint8)
    else:
        c = by_word.astype(ml_dtypes.float4_e2m1fn).view(np.uint8) & 0xF
        words = c[..., 0::2] | (c[..., 1::2] << 4)
    return np.ascontiguousarray(words), np.ascontiguousarray(byte.astype(np.uint8).reshape(k // 512, 16, n))


def unpack_weight(words, scales, fmt):
    g, p, n, _ = words.shape
    if fmt == "e4m3":
        vals = np.ascontiguousarray(words).view(ml_dtypes.float8_e4m3fn).astype(np.float64)
    else:
        nib = np.empty((g, p, n, 4), np.uint8)
        nib[..., 0::2] = words & 0xF
        nib[..., 1::2] = words >> 4
        vals = E2M1[nib]
    vals = vals * np.repeat(np.exp2(scales.astype(np.float64) - 127.0), 8, axis=1)[..., None]
    return vals.transpose(0, 1, 3, 2).reshape(g * 512, n)

def pack4(w):
    words, scales = pack_weight(w, "e2m1")
    return words.reshape(words.shape[0], 128, -1), scales


def unpack4(words, scales):
    return unpack_weight(words.reshape(words.shape[0], 128, -1, 2), scales, "e2m1")


B, F, H, W, D, NH, PF, PH, PW, CF, TF, LR = 1, 40, 8, 8, 512, 4, 8, 4, 4, 6, 5, 18
S = F * H * W
HD = D // NH
EPS = 1e-5


def rms_norm(y, g):
    v = np.mean(np.square(y), axis=-1, keepdims=True)
    return y / np.sqrt(v + EPS) * g


def rope(y, freqs):
    yr = y.reshape(B, S, NH, HD // 2, 2)
    c, s = freqs[..., 0], freqs[..., 1]
    a, d = yr[..., 0], yr[..., 1]
    return np.stack([a * c - d * s, a * s + d * c], axis=-1).reshape(B, S, D)


def window_order(y):
    y = y.reshape(B, F // PF, PF, H // PH, PH, W // PW, PW, D)
    return y.transpose(0, 1, 3, 5, 2, 4, 6, 7).reshape(B, S, D)


def setup_inputs():
    s = mx_kscale(D)
    ang = np.random.uniform(0.0, 2.0 * np.pi, (S, 1, HD // 2))
    x = bf(np.random.standard_normal((B, S, D)) * s)
    freqs = bf(np.stack([np.cos(ang), np.sin(ang)], axis=-1))
    w_words, w_scales = pack4(np.random.standard_normal((D, D)) / np.sqrt(D) / s[:, None])
    b = bf(0.1 * np.random.standard_normal(D))
    g = bf(1.0 + 0.1 * np.random.standard_normal(D))
    return {"x": x,
            "freqs": freqs,
            "w_words": w_words,
            "w_scales": w_scales,
            "b": b,
            "g": g}


def reference(x, freqs, w_words, w_scales, b, g):
    y = (mxq(f64(x), 2, "e5m2") @ unpack4(w_words, w_scales)) + f64(b)
    return window_order(rope(rms_norm(y, f64(g)), f64(freqs)))

@@ -1,0 +1,323 @@
+from contextlib import ExitStack
+
+import concourse.mybir as mybir
+from concourse.masks import make_identity
+
+F32 = mybir.dt.float32
+BF16 = mybir.dt.bfloat16
+I32 = mybir.dt.int32
+U32 = mybir.dt.uint32
+U8 = mybir.dt.uint8
+E5M2X4 = mybir.dt.float8_e5m2_x4
+E2M1X4 = mybir.dt.float4_e2m1fn_x4
+ACT = mybir.ActivationFunctionType
+ALU = mybir.AluOpType
+
+P = 128
+S, D = 2560, 512
+HEADS, PAIRS = 4, 64
+EPS = 1e-5
+FLOPS = 2 * S * D * D
+
+SIZES = [1] + [2] * 9 + [1]
+GROUPS = [(sum(SIZES[:i]), n) for i, n in enumerate(SIZES)]
+FIRST_SCALAR_COPY_GROUP = 5
+HEAD_FRONTS = 5
+
+
+def tile_selfattention_pa_kernel(tc, x, freqs, w_words, w_scales, b, g, out):
+    nc = tc.nc
+    n_groups = len(GROUPS)
+    x_rows = x[0].rearrange("(fo q wi) d -> fo q wi d", q=P, wi=4)
+    out_rows = out[0].rearrange("(fo p wi) d -> fo p wi d", p=P, wi=4)
+    freq_rows = freqs.rearrange(
+        "(fo fi ho hi wo wi) o j e -> fo ho wo fi hi (wi o j e)", fi=8, ho=2, hi=4, wo=2, wi=4
+    )
+
+    with ExitStack() as ctx:
+        keep = ctx.enter_context(tc.tile_pool(name="keep", bufs=1))
+        work = ctx.enter_context(tc.tile_pool(name="work", bufs=3))
+        psum = ctx.enter_context(tc.psum_pool(name="psum", bufs=2))
+        ctx.enter_context(tc.manual_schedule())
+
+        ident = keep.tile([P, P], F32, name="ident")
+        perm = keep.tile([P, P], F32, name="perm")
+        words = keep.tile([P, 2 * D], U8, name="words", align_bytes=64)
+        plane = keep.tile([P, 4, D], U8, name="plane", align_bytes=64)
+        bg_rows = keep.tile([8, P], BF16, name="bg_rows")
+        bg_square = keep.tile([P, P], F32, name="bg_square")
+        bg = keep.tile([P, 8], F32, name="bg")
+        gb = keep.tile([P, HEADS], F32, name="gb")
+
+        x_sb, grouped, codes, scales, fr = {}, {}, {}, {}, {}
+        mm_pair = {}
+        xt_bank, mm_bank, ss_bank, u_bank = {}, {}, {}, {}
+        u_sb, sq_sb, ssum, std, rstd, t1, t2 = {}, {}, {}, {}, {}, {}, {}
+
+        def load_x(fo, w0, n):
+            rows = keep.tile([P, n, D], BF16, name="x%d_%d" % (fo, w0))
+            nc.sync.dma_start(out=rows[:], in_=x_rows[fo, :, w0 : w0 + n, :])
+            for w in range(n):
+                x_sb[4 * fo + w0 + w] = rows[:, w, :]
+
+        def load_freqs(fo):
+            fr[fo] = keep.tile([P, 4, 2 * PAIRS], BF16, name="fr%d" % fo)
+            flat = fr[fo][:].rearrange("p w m -> p (w m)")
+            for ho in range(2):
+                for wo in range(2):
+                    p0 = 64 * ho + 32 * wo
+                    nc.sync.dma_start(out=flat[p0 : p0 + 32, :], in_=freq_rows[fo, ho, wo])
+
+        def transpose_x(i, half):
+            t0, n = GROUPS[i]
+            bank = psum.tile([P, 2, 2, P], F32, name="xt_bank", tag="u", bufs=3)
+            xt_bank[i, half] = bank
+            for w in range(2 * half, min(n, 2 * half + 2)):
+                x_words = x_sb[t0 + w].bitcast(F32)
+                for u in range(2):
+                    nc.tensor.transpose(bank[:, w - 2 * half, u, :], x_words[:, u : 256 : 2], perm[:])
+
+        def copy_x(i, half):
+            n = GROUPS[i][1]
+            if half == 0:
+                grouped[i] = keep.tile([P, n * D], BF16, name="grouped%d" % i, align_bytes=64)
+            m = min(n - 2 * half, 2)
+            dst = grouped[i][:, 2 * half * D : (2 * half + m) * D].bitcast(F32)
+            dst = dst.rearrange("p (t r u) -> p t r u", r=P, u=2)
+            src = xt_bank[i, half][:, 0:m, :, :].rearrange("p t u r -> p t r u")
+            if i >= FIRST_SCALAR_COPY_GROUP:
+                nc.scalar.copy(out=dst, in_=src)
+            else:
+                nc.vector.tensor_copy(out=dst, in_=src)
+
+        def quantize(i):
+            n = GROUPS[i][1]
+            codes[i] = keep.tile([P, n * P], U32, name="codes%d" % i, align_bytes=64)
+            scales[i] = keep.tile([P, n * P], U8, name="scales%d" % i, align_bytes=64)
+            nc.vector.quantize_mx(out=codes[i][:].bitcast(E5M2X4), scales=scales[i][:], in_=grouped[i][:])
+
+        def project(i, c):
+            n = GROUPS[i][1]
+            if c % 2 == 0:
+                mm_pair[i, c // 2] = psum.tile([P, 2, 2 * P], F32, name="mm_bank", tag="mm", bufs=4)
+            mm_bank[i, c] = mm_pair[i, c // 2][:, c % 2, :]
+            nc.tensor.matmul_mx(
+                out=mm_bank[i, c][:, : n * P],
+                lhsT=words[:, 2 * P * c : 2 * P * (c + 1)].bitcast(E2M1X4),
+                lhsT_scale=plane[:, 0, P * c : P * (c + 1)],
+                rhs=codes[i][:].bitcast(E5M2X4),
+                rhs_scale=scales[i][:],
+                start=True,
+                stop=True,
+            )
+
+        def square(i, c):
+            n = GROUPS[i][1]
+            if c == 0:
+                u_sb[i] = work.tile([P, HEADS, D], F32, name="u_sb")
+                sq_sb[i] = work.tile([P, HEADS, D], F32, name="sq_sb", bufs=2)
+            src = mm_bank[i, c][:, : n * P]
+            nc.scalar.activation(out=sq_sb[i][:, c, : n * P], in_=src, func=ACT.Square, bias=bg[:, c : c + 1])
+
+        def gain(i, c):
+            n = GROUPS[i][1]
+            nc.scalar.activation(
+                out=u_sb[i][:, c, : n * P],
+                in_=mm_bank[i, c][:, : n * P],
+                func=ACT.Identity,
+                bias=gb[:, c : c + 1],
+                scale=bg[:, HEADS + c : HEADS + c + 1],
+            )
+
+        def transpose_squares(i, c):
+            n = GROUPS[i][1]
+            if c == 0:
+                ss_bank[i] = psum.tile([P, 4, P], F32, name="ss_bank", tag="ss", bufs=1)
+            for w in range(n):
+                nc.tensor.matmul(
+                    out=ss_bank[i][:, w, :],
+                    lhsT=sq_sb[i][:, c, w * P : (w + 1) * P],
+                    rhs=ident[:],
+                    is_transpose=True,
+                    start=(c == 0 and w == 0),
+                    stop=(c == HEADS - 1 and w == n - 1),
+                )
+
+        def sum_squares(i):
+            n = GROUPS[i][1]
+            ssum[i] = keep.tile([P, n], F32, name="ssum%d" % i)
+            nc.vector.tensor_reduce(out=ssum[i][:], in_=ss_bank[i][:, :n, :], axis=mybir.AxisListType.X, op=ALU.add)
+
+        def root(i):
+            n = GROUPS[i][1]
+            std[i] = keep.tile([P, 2, n], F32, name="std%d" % i)
+            nc.scalar.activation(out=std[i][:, 0, :], in_=ssum[i][:], func=ACT.Sqrt, scale=1.0 / D, bias=EPS)
+
+        def negate_root(i):
+            nc.scalar.activation(out=std[i][:, 1, :], in_=std[i][:, 0, :], func=ACT.Copy, scale=-1.0)
+
+        def invert(i):
+            n = GROUPS[i][1]
+            rstd[i] = keep.tile([P, 2, n], F32, name="rstd%d" % i)
+            nc.vector.reciprocal(out=rstd[i][:], in_=std[i][:])
+
+        def transpose_u(i, w):
+            bank = psum.tile([P, HEADS, P], F32, name="u_bank", tag="u", bufs=3)
+            u_bank[i, w] = bank
+            for c in range(HEADS):
+                nc.tensor.transpose(bank[:, c, :], u_sb[i][:, c, w * P : (w + 1) * P], ident[:])
+
+        def rope_first(i, w):
+            t0, n = GROUPS[i]
+            t1[i, w] = work.tile([P, D], F32, name="t1", bufs=5)
+            t2[i, w] = work.tile([P, D], F32, name="t2", bufs=5)
+            u_split = u_bank[i, w][:].rearrange("p h (j e) -> p e h j", e=2)
+            cs = fr[(t0 + w) // 4][:, (t0 + w) % 4, :].rearrange("p (j e) -> p e j", e=2)
+            cos = cs[:, 0:1, :].to_broadcast([P, 2 * HEADS, PAIRS])
+            sin = cs[:, 1:2, :].to_broadcast([P, HEADS, PAIRS])
+            nc.vector.scalar_tensor_tensor(
+                out=t1[i, w][:].rearrange("p (m j) -> p m j", j=PAIRS),
+                in0=u_split,
+                scalar=rstd[i][:, 0, w : w + 1],
+                in1=cos,
+                op0=ALU.mult,
+                op1=ALU.mult,
+            )
+            nc.vector.scalar_tensor_tensor(
+                out=t2[i, w][:, : D // 2].rearrange("p (h j) -> p h j", h=HEADS),
+                in0=u_split[:, 1, :, :],
+                scalar=rstd[i][:, 1, w : w + 1],
+                in1=sin,
+                op0=ALU.mult,
+                op1=ALU.mult,
+            )
+
+        def rope_second(i, w):
+            t0, n = GROUPS[i]
+            u_split = u_bank[i, w][:].rearrange("p h (j e) -> p e h j", e=2)
+            cs = fr[(t0 + w) // 4][:, (t0 + w) % 4, :].rearrange("p (j e) -> p e j", e=2)
+            sin = cs[:, 1:2, :].to_broadcast([P, HEADS, PAIRS])
+            nc.vector.scalar_tensor_tensor(
+                out=t2[i, w][:, D // 2 :].rearrange("p (h j) -> p h j", h=HEADS),
+                in0=u_split[:, 0, :, :],
+                scalar=rstd[i][:, 0, w : w + 1],
+                in1=sin,
+                op0=ALU.mult,
+                op1=ALU.mult,
+            )
+
+        def rope(i, w):
+            rope_first(i, w)
+            rope_second(i, w)
+
+        def add_and_store(i, w):
+            t0, n = GROUPS[i]
+            res = work.tile([P, D], F32, name="res", bufs=6)
+            engine = nc.vector if i == n_groups - 1 else nc.gpsimd
+            engine.tensor_tensor(
+                out=res[:].rearrange("p (k e) -> p k e", e=2),
+                in0=t1[i, w][:].rearrange("p (e k) -> p k e", e=2),
+                in1=t2[i, w][:].rearrange("p (e k) -> p k e", e=2),
+                op=ALU.add,
+            )
+            fo, wi = divmod(t0 + w, 4)
+            nc.sync.dma_start(out=out_rows[fo, :, wi, :], in_=res[:])
+
+        make_identity(nc, ident[:])
+        load_x(0, 0, 1)
+        nc.scalar.dma_start(out=bg_rows[0:4, :], in_=b.rearrange("(c m) -> c m", m=P))
+        nc.scalar.dma_start(out=bg_rows[4:8, :], in_=g.rearrange("(c m) -> c m", m=P))
+        nc.sync.dma_start(
+            out=plane[0:4, :, :].bitcast(I32), in_=w_scales[0].rearrange("(q r) n -> r q n", r=4).bitcast(I32)
+        )
+        nc.sync.dma_start(out=words[:].bitcast(I32), in_=w_words[0].bitcast(I32))
+        load_x(0, 1, 3)
+        load_x(1, 0, 4)
+        load_freqs(0)
+        for fo in range(2, 5):
+            load_x(fo, 0, 4)
+            load_freqs(fo - 1)
+        load_freqs(4)
+        nc.vector.memset(bg_square[:], 0.0)
+        ident_split = ident[:].rearrange("r (fi ho hi wo) -> r ho wo fi hi", fi=8, ho=2, hi=4)
+        perm_split = perm[:].rearrange("r (ho wo fi hi) -> r ho wo fi hi", ho=2, wo=2, fi=8)
+        for ho in range(2):
+            nc.vector.tensor_copy(out=perm_split[:, ho], in_=ident_split[:, ho])
+        nc.vector.tensor_copy(out=bg_square[0:8, :], in_=bg_rows[:])
+        for q in range(1, 4):
+            nc.vector.tensor_copy(out=plane[32 * q : 32 * q + 4, 0, :].bitcast(I32), in_=plane[0:4, q, :].bitcast(I32))
+
+        transpose_x(0, 0)
+        bg_bank = psum.tile([P, 4, P], F32, name="bg_bank", tag="ss", bufs=1)
+        nc.tensor.transpose(bg_bank[:, 0, :], bg_square[:], ident[:])
+        copy_x(0, 0)
+        nc.vector.tensor_copy(out=bg[:], in_=bg_bank[:, 0, 0:8])
+        quantize(0)
+        nc.vector.tensor_tensor(out=gb[:], in0=bg[:, 0:HEADS], in1=bg[:, HEADS:8], op=ALU.mult)
+
+        def project_all(i):
+            for c in range(HEADS):
+                project(i, c)
+
+        def square_and_gain(i, c):
+            square(i, c)
+            gain(i, c)
+
+        transpose_x(1, 0)
+        project_all(0)
+        copy_x(1, 0)
+        transpose_x(2, 0)
+        quantize(1)
+        project_all(1)
+        transpose_x(3, 0)
+        for c in range(HEADS):
+            square_and_gain(0, c)
+        copy_x(2, 0)
+        quantize(2)
+        copy_x(3, 0)
+
+        for a in range(-1, n_groups):
+            mid, nxt, far, f = a + 1, a + 2, a + 3, a + 5
+            n_a = GROUPS[a][1] if a >= 0 else 0
+            has_mid = mid < n_groups
+            has_nxt = nxt < n_groups
+            has_f = f < n_groups
+            if n_a > 1:
+                transpose_u(a, 1)
+            if n_a > 0:
+                rope(a, 0)
+                add_and_store(a, 0)
+            if has_mid:
+                for c in range(HEADS):
+                    transpose_squares(mid, c)
+                sum_squares(mid)
+                transpose_u(mid, 0)
+            if has_nxt:
+                square_and_gain(nxt, 0)
+                square_and_gain(nxt, 1)
+            if far < n_groups:
+                project_all(far)
+            if has_f:
+                transpose_x(f, 0)
+            if has_mid:
+                root(mid)
+            if has_nxt:
+                square(nxt, 2)
+            if has_mid:
+                negate_root(mid)
+            if has_nxt:
+                gain(nxt, 2)
+                square_and_gain(nxt, 3)
+            if n_a > 1:
+                rope_first(a, 1)
+            if has_f and f < FIRST_SCALAR_COPY_GROUP:
+                copy_x(f, 0)
+            if has_mid:
+                invert(mid)
+            if f - 1 < n_groups:
+                quantize(f - 1)
+            if n_a > 1:
+                rope_second(a, 1)
+                add_and_store(a, 1)
+            if has_f and f >= FIRST_SCALAR_COPY_GROUP:
+                copy_x(f, 0)

@@ -21,7 +21,7 @@ FLOPS = 2 * S * D * D
 
 SIZES = [1] + [2] * 9 + [1]
 GROUPS = [(sum(SIZES[:i]), n) for i, n in enumerate(SIZES)]
-FIRST_SCALAR_COPY_GROUP = 5
+FIRST_SCALAR_COPY_GROUP = 4
 HEAD_FRONTS = 5
 
 
@@ -169,14 +169,15 @@ def tile_selfattention_pa_kernel(tc, x, freqs, w_words, w_scales, b, g, out):
 
         def rope_first(i, w):
             t0, n = GROUPS[i]
-            t1[i, w] = work.tile([P, D], F32, name="t1", bufs=5)
-            t2[i, w] = work.tile([P, D], F32, name="t2", bufs=5)
+            if w == 0:
+                t1[i] = work.tile([P, 2, 2, D // 2], F32, name="t1")
+                t2[i] = work.tile([P, 2, 2, D // 2], F32, name="t2")
             u_split = u_bank[i, w][:].rearrange("p h (j e) -> p e h j", e=2)
             cs = fr[(t0 + w) // 4][:, (t0 + w) % 4, :].rearrange("p (j e) -> p e j", e=2)
             cos = cs[:, 0:1, :].to_broadcast([P, 2 * HEADS, PAIRS])
             sin = cs[:, 1:2, :].to_broadcast([P, HEADS, PAIRS])
             nc.vector.scalar_tensor_tensor(
-                out=t1[i, w][:].rearrange("p (m j) -> p m j", j=PAIRS),
+                out=t1[i][:, :, w, :],
                 in0=u_split,
                 scalar=rstd[i][:, 0, w : w + 1],
                 in1=cos,
@@ -184,7 +185,7 @@ def tile_selfattention_pa_kernel(tc, x, freqs, w_words, w_scales, b, g, out):
                 op1=ALU.mult,
             )
             nc.vector.scalar_tensor_tensor(
-                out=t2[i, w][:, : D // 2].rearrange("p (h j) -> p h j", h=HEADS),
+                out=t2[i][:, 0, w, :].rearrange("p (h j) -> p h j", h=HEADS),
                 in0=u_split[:, 1, :, :],
                 scalar=rstd[i][:, 1, w : w + 1],
                 in1=sin,
@@ -198,7 +199,7 @@ def tile_selfattention_pa_kernel(tc, x, freqs, w_words, w_scales, b, g, out):
             cs = fr[(t0 + w) // 4][:, (t0 + w) % 4, :].rearrange("p (j e) -> p e j", e=2)
             sin = cs[:, 1:2, :].to_broadcast([P, HEADS, PAIRS])
             nc.vector.scalar_tensor_tensor(
-                out=t2[i, w][:, D // 2 :].rearrange("p (h j) -> p h j", h=HEADS),
+                out=t2[i][:, 1, w, :].rearrange("p (h j) -> p h j", h=HEADS),
                 in0=u_split[:, 0, :, :],
                 scalar=rstd[i][:, 0, w : w + 1],
                 in1=sin,
@@ -210,18 +211,18 @@ def tile_selfattention_pa_kernel(tc, x, freqs, w_words, w_scales, b, g, out):
             rope_first(i, w)
             rope_second(i, w)
 
-        def add_and_store(i, w):
-            t0, n = GROUPS[i]
-            res = work.tile([P, D], F32, name="res", bufs=6)
-            engine = nc.vector if i == n_groups - 1 else nc.gpsimd
+        def add_and_store(engine, i, w0, m):
+            t0 = GROUPS[i][0]
+            res = work.tile([P, 2, D], F32, name="res", bufs=4)
             engine.tensor_tensor(
-                out=res[:].rearrange("p (k e) -> p k e", e=2),
-                in0=t1[i, w][:].rearrange("p (e k) -> p k e", e=2),
-                in1=t2[i, w][:].rearrange("p (e k) -> p k e", e=2),
+                out=res[:, :m, :].rearrange("p t (k i e) -> p (t k) e i", i=2, e=2),
+                in0=t1[i][:, :, w0 : w0 + m, :].rearrange("p e t (k i) -> p (t k) e i", i=2),
+                in1=t2[i][:, :, w0 : w0 + m, :].rearrange("p e t (k i) -> p (t k) e i", i=2),
                 op=ALU.add,
             )
-            fo, wi = divmod(t0 + w, 4)
-            nc.sync.dma_start(out=out_rows[fo, :, wi, :], in_=res[:])
+            for w in range(m):
+                fo, wi = divmod(t0 + w0 + w, 4)
+                nc.sync.dma_start(out=out_rows[fo, :, wi, :], in_=res[:, w, :])
 
         make_identity(nc, ident[:])
         load_x(0, 0, 1)
@@ -286,7 +287,8 @@ def tile_selfattention_pa_kernel(tc, x, freqs, w_words, w_scales, b, g, out):
                 transpose_u(a, 1)
             if n_a > 0:
                 rope(a, 0)
-                add_and_store(a, 0)
+            if a == n_groups - 2:
+                add_and_store(nc.gpsimd, a, 0, 1)
             if has_mid:
                 for c in range(HEADS):
                     transpose_squares(mid, c)
@@ -318,6 +320,10 @@ def tile_selfattention_pa_kernel(tc, x, freqs, w_words, w_scales, b, g, out):
                 quantize(f - 1)
             if n_a > 1:
                 rope_second(a, 1)
-                add_and_store(a, 1)
+            if 0 <= a < n_groups - 2:
+                add_and_store(nc.gpsimd, a, 0, n_a)
             if has_f and f >= FIRST_SCALAR_COPY_GROUP:
                 copy_x(f, 0)
+
+        add_and_store(nc.vector, n_groups - 2, 1, 1)
+        add_and_store(nc.vector, n_groups - 1, 0, 1)

@@ -22,7 +22,8 @@ FLOPS = 2 * S * D * D
 SIZES = [1] + [2] * 9 + [1]
 GROUPS = [(sum(SIZES[:i]), n) for i, n in enumerate(SIZES)]
 FIRST_SCALAR_COPY_GROUP = 4
-HEAD_FRONTS = 5
+TABLE_STEPS = {-1: 1, 0: 2, 5: 3, 7: 4}
+COS_V = 3
 
 
 def tile_selfattention_pa_kernel(tc, x, freqs, w_words, w_scales, b, g, out):
@@ -50,7 +51,7 @@ def tile_selfattention_pa_kernel(tc, x, freqs, w_words, w_scales, b, g, out):
         gb = keep.tile([P, HEADS], F32, name="gb")
 
         x_sb, grouped, codes, scales, fr = {}, {}, {}, {}, {}
-        mm_pair = {}
+        mm_pair, cos2, sin2 = {}, {}, {}
         xt_bank, mm_bank, ss_bank, u_bank = {}, {}, {}, {}
         u_sb, sq_sb, ssum, std, rstd, t1, t2 = {}, {}, {}, {}, {}, {}, {}
 
@@ -150,15 +151,12 @@ def tile_selfattention_pa_kernel(tc, x, freqs, w_words, w_scales, b, g, out):
 
         def root(i):
             n = GROUPS[i][1]
-            std[i] = keep.tile([P, 2, n], F32, name="std%d" % i)
-            nc.scalar.activation(out=std[i][:, 0, :], in_=ssum[i][:], func=ACT.Sqrt, scale=1.0 / D, bias=EPS)
-
-        def negate_root(i):
-            nc.scalar.activation(out=std[i][:, 1, :], in_=std[i][:, 0, :], func=ACT.Copy, scale=-1.0)
+            std[i] = keep.tile([P, n], F32, name="std%d" % i)
+            nc.scalar.activation(out=std[i][:], in_=ssum[i][:], func=ACT.Sqrt, scale=1.0 / D, bias=EPS)
 
         def invert(i):
             n = GROUPS[i][1]
-            rstd[i] = keep.tile([P, 2, n], F32, name="rstd%d" % i)
+            rstd[i] = keep.tile([P, n], F32, name="rstd%d" % i)
             nc.vector.reciprocal(out=rstd[i][:], in_=std[i][:])
 
         def transpose_u(i, w):
@@ -167,42 +165,43 @@ def tile_selfattention_pa_kernel(tc, x, freqs, w_words, w_scales, b, g, out):
             for c in range(HEADS):
                 nc.tensor.transpose(bank[:, c, :], u_sb[i][:, c, w * P : (w + 1) * P], ident[:])
 
+        def build_tables(fo):
+            pairs = fr[fo][:].rearrange("p w (j e) -> p (w j) e", e=2)
+            cos2[fo] = keep.tile([P, 4, 2 * PAIRS], BF16, name="cos2_%d" % fo)
+            sin2[fo] = keep.tile([P, 4, 2 * PAIRS], BF16, name="sin2_%d" % fo)
+            nc.vector.tensor_copy(out=sin2[fo][:], in_=fr[fo][:])
+            cos_copy = nc.vector.tensor_copy if fo < COS_V else nc.scalar.copy
+            cos_copy(
+                out=cos2[fo][:].rearrange("p w (j e) -> p (w j) e", e=2),
+                in_=pairs[:, :, 0:1].to_broadcast([P, 4 * PAIRS, 2]),
+            )
+            nc.vector.tensor_scalar_mul(
+                sin2[fo][:].rearrange("p w (j e) -> p (w j) e", e=2)[:, :, 0], pairs[:, :, 1], -1.0
+            )
+
         def rope_first(i, w):
             t0, n = GROUPS[i]
+            fo, wi = divmod(t0 + w, 4)
             if w == 0:
-                t1[i] = work.tile([P, 2, 2, D // 2], F32, name="t1")
-                t2[i] = work.tile([P, 2, 2, D // 2], F32, name="t2")
-            u_split = u_bank[i, w][:].rearrange("p h (j e) -> p e h j", e=2)
-            cs = fr[(t0 + w) // 4][:, (t0 + w) % 4, :].rearrange("p (j e) -> p e j", e=2)
-            cos = cs[:, 0:1, :].to_broadcast([P, 2 * HEADS, PAIRS])
-            sin = cs[:, 1:2, :].to_broadcast([P, HEADS, PAIRS])
+                t1[i] = work.tile([P, 2, D], F32, name="t1")
+                t2[i] = work.tile([P, 2, D], F32, name="t2")
             nc.vector.scalar_tensor_tensor(
-                out=t1[i][:, :, w, :],
-                in0=u_split,
-                scalar=rstd[i][:, 0, w : w + 1],
-                in1=cos,
-                op0=ALU.mult,
-                op1=ALU.mult,
-            )
-            nc.vector.scalar_tensor_tensor(
-                out=t2[i][:, 0, w, :].rearrange("p (h j) -> p h j", h=HEADS),
-                in0=u_split[:, 1, :, :],
-                scalar=rstd[i][:, 1, w : w + 1],
-                in1=sin,
+                out=t1[i][:, w, :].rearrange("p (h m) -> p h m", h=HEADS),
+                in0=cos2[fo][:, wi : wi + 1, :].to_broadcast([P, HEADS, 2 * PAIRS]),
+                scalar=rstd[i][:, w : w + 1],
+                in1=u_bank[i, w][:],
                 op0=ALU.mult,
                 op1=ALU.mult,
             )
 
         def rope_second(i, w):
             t0, n = GROUPS[i]
-            u_split = u_bank[i, w][:].rearrange("p h (j e) -> p e h j", e=2)
-            cs = fr[(t0 + w) // 4][:, (t0 + w) % 4, :].rearrange("p (j e) -> p e j", e=2)
-            sin = cs[:, 1:2, :].to_broadcast([P, HEADS, PAIRS])
+            fo, wi = divmod(t0 + w, 4)
             nc.vector.scalar_tensor_tensor(
-                out=t2[i][:, 1, w, :].rearrange("p (h j) -> p h j", h=HEADS),
-                in0=u_split[:, 0, :, :],
-                scalar=rstd[i][:, 0, w : w + 1],
-                in1=sin,
+                out=t2[i][:, w, :].rearrange("p (h m) -> p h m", h=HEADS),
+                in0=sin2[fo][:, wi : wi + 1, :].to_broadcast([P, HEADS, 2 * PAIRS]),
+                scalar=rstd[i][:, w : w + 1],
+                in1=u_bank[i, w][:].rearrange("p h (j e) -> p (h j) e", e=2)[:, :, ::-1],
                 op0=ALU.mult,
                 op1=ALU.mult,
             )
@@ -215,9 +214,9 @@ def tile_selfattention_pa_kernel(tc, x, freqs, w_words, w_scales, b, g, out):
             t0 = GROUPS[i][0]
             res = work.tile([P, 2, D], F32, name="res", bufs=4)
             engine.tensor_tensor(
-                out=res[:, :m, :].rearrange("p t (k i e) -> p (t k) e i", i=2, e=2),
-                in0=t1[i][:, :, w0 : w0 + m, :].rearrange("p e t (k i) -> p (t k) e i", i=2),
-                in1=t2[i][:, :, w0 : w0 + m, :].rearrange("p e t (k i) -> p (t k) e i", i=2),
+                out=res[:, :m, :],
+                in0=t1[i][:, w0 : w0 + m, :],
+                in1=t2[i][:, w0 : w0 + m, :],
                 op=ALU.add,
             )
             for w in range(m):
@@ -275,6 +274,7 @@ def tile_selfattention_pa_kernel(tc, x, freqs, w_words, w_scales, b, g, out):
             square_and_gain(0, c)
         copy_x(2, 0)
         quantize(2)
+        build_tables(0)
         copy_x(3, 0)
 
         for a in range(-1, n_groups):
@@ -283,6 +283,9 @@ def tile_selfattention_pa_kernel(tc, x, freqs, w_words, w_scales, b, g, out):
             has_mid = mid < n_groups
             has_nxt = nxt < n_groups
             has_f = f < n_groups
+            if has_mid:
+                for c in range(HEADS):
+                    transpose_squares(mid, c)
             if n_a > 1:
                 transpose_u(a, 1)
             if n_a > 0:
@@ -290,8 +293,6 @@ def tile_selfattention_pa_kernel(tc, x, freqs, w_words, w_scales, b, g, out):
             if a == n_groups - 2:
                 add_and_store(nc.gpsimd, a, 0, 1)
             if has_mid:
-                for c in range(HEADS):
-                    transpose_squares(mid, c)
                 sum_squares(mid)
                 transpose_u(mid, 0)
             if has_nxt:
@@ -305,21 +306,19 @@ def tile_selfattention_pa_kernel(tc, x, freqs, w_words, w_scales, b, g, out):
                 root(mid)
             if has_nxt:
                 square(nxt, 2)
-            if has_mid:
-                negate_root(mid)
             if has_nxt:
                 gain(nxt, 2)
                 square_and_gain(nxt, 3)
             if n_a > 1:
-                rope_first(a, 1)
+                rope(a, 1)
             if has_f and f < FIRST_SCALAR_COPY_GROUP:
                 copy_x(f, 0)
             if has_mid:
                 invert(mid)
             if f - 1 < n_groups:
                 quantize(f - 1)
-            if n_a > 1:
-                rope_second(a, 1)
+            if a in TABLE_STEPS:
+                build_tables(TABLE_STEPS[a])
             if 0 <= a < n_groups - 2:
                 add_and_store(nc.gpsimd, a, 0, n_a)
             if has_f and f >= FIRST_SCALAR_COPY_GROUP:

@@ -22,8 +22,10 @@ FLOPS = 2 * S * D * D
 SIZES = [1] + [2] * 9 + [1]
 GROUPS = [(sum(SIZES[:i]), n) for i, n in enumerate(SIZES)]
 FIRST_SCALAR_COPY_GROUP = 4
-TABLE_STEPS = {-1: 1, 0: 2, 5: 3, 7: 4}
-COS_V = 3
+TABLE_STEPS = {-1: 1, 0: 2, 1: 3, 2: 4}
+PLAIN = (4, 5)
+SCALE_S = 6
+SCALE_BOTH = 8
 
 
 def tile_selfattention_pa_kernel(tc, x, freqs, w_words, w_scales, b, g, out):
@@ -51,7 +53,7 @@ def tile_selfattention_pa_kernel(tc, x, freqs, w_words, w_scales, b, g, out):
         gb = keep.tile([P, HEADS], F32, name="gb")
 
         x_sb, grouped, codes, scales, fr = {}, {}, {}, {}, {}
-        mm_pair, cos2, sin2 = {}, {}, {}
+        mm_pair, scaled = {}, {}
         xt_bank, mm_bank, ss_bank, u_bank = {}, {}, {}, {}
         u_sb, sq_sb, ssum, std, rstd, t1, t2 = {}, {}, {}, {}, {}, {}, {}
 
@@ -62,8 +64,8 @@ def tile_selfattention_pa_kernel(tc, x, freqs, w_words, w_scales, b, g, out):
                 x_sb[4 * fo + w0 + w] = rows[:, w, :]
 
         def load_freqs(fo):
-            fr[fo] = keep.tile([P, 4, 2 * PAIRS], BF16, name="fr%d" % fo)
-            flat = fr[fo][:].rearrange("p w m -> p (w m)")
+            fr[fo] = keep.tile([P, 2, 4, 2 * PAIRS], BF16, name="fr%d" % fo)
+            flat = fr[fo][:, 1].rearrange("p w m -> p (w m)")
             for ho in range(2):
                 for wo in range(2):
                     p0 = 64 * ho + 32 * wo
@@ -139,7 +141,7 @@ def tile_selfattention_pa_kernel(tc, x, freqs, w_words, w_scales, b, g, out):
                     out=ss_bank[i][:, w, :],
                     lhsT=sq_sb[i][:, c, w * P : (w + 1) * P],
                     rhs=ident[:],
-                    is_transpose=True,
+                    is_transpose=(c * n + w not in PLAIN),
                     start=(c == 0 and w == 0),
                     stop=(c == HEADS - 1 and w == n - 1),
                 )
@@ -149,15 +151,10 @@ def tile_selfattention_pa_kernel(tc, x, freqs, w_words, w_scales, b, g, out):
             ssum[i] = keep.tile([P, n], F32, name="ssum%d" % i)
             nc.vector.tensor_reduce(out=ssum[i][:], in_=ss_bank[i][:, :n, :], axis=mybir.AxisListType.X, op=ALU.add)
 
-        def root(i):
-            n = GROUPS[i][1]
-            std[i] = keep.tile([P, n], F32, name="std%d" % i)
-            nc.scalar.activation(out=std[i][:], in_=ssum[i][:], func=ACT.Sqrt, scale=1.0 / D, bias=EPS)
-
-        def invert(i):
+        def inverse_root(i):
             n = GROUPS[i][1]
             rstd[i] = keep.tile([P, n], F32, name="rstd%d" % i)
-            nc.vector.reciprocal(out=rstd[i][:], in_=std[i][:])
+            nc.scalar.activation(out=rstd[i][:], in_=ssum[i][:], func=ACT.Abs_reciprocal_sqrt, scale=1.0 / D, bias=EPS)
 
         def transpose_u(i, w):
             bank = psum.tile([P, HEADS, P], F32, name="u_bank", tag="u", bufs=3)
@@ -165,50 +162,39 @@ def tile_selfattention_pa_kernel(tc, x, freqs, w_words, w_scales, b, g, out):
             for c in range(HEADS):
                 nc.tensor.transpose(bank[:, c, :], u_sb[i][:, c, w * P : (w + 1) * P], ident[:])
 
-        def build_tables(fo):
-            pairs = fr[fo][:].rearrange("p w (j e) -> p (w j) e", e=2)
-            cos2[fo] = keep.tile([P, 4, 2 * PAIRS], BF16, name="cos2_%d" % fo)
-            sin2[fo] = keep.tile([P, 4, 2 * PAIRS], BF16, name="sin2_%d" % fo)
-            nc.vector.tensor_copy(out=sin2[fo][:], in_=fr[fo][:])
-            cos_copy = nc.vector.tensor_copy if fo < COS_V else nc.scalar.copy
-            cos_copy(
-                out=cos2[fo][:].rearrange("p w (j e) -> p (w j) e", e=2),
-                in_=pairs[:, :, 0:1].to_broadcast([P, 4 * PAIRS, 2]),
-            )
-            nc.vector.tensor_scalar_mul(
-                sin2[fo][:].rearrange("p w (j e) -> p (w j) e", e=2)[:, :, 0], pairs[:, :, 1], -1.0
-            )
+        def negate_freqs(fo):
+            nc.vector.tensor_scalar_mul(fr[fo][:, 0], fr[fo][:, 1], -1.0)
 
-        def rope_first(i, w):
-            t0, n = GROUPS[i]
-            fo, wi = divmod(t0 + w, 4)
+        def on_scalar(i, w):
+            return (w == 1 and i >= SCALE_S) or i >= SCALE_BOTH
+
+        def scale_freqs(i, w):
+            fo, wi = divmod(GROUPS[i][0] + w, 4)
+            scaled[i, w] = work.tile([P, 2, 2 * PAIRS], F32, name="scaled", bufs=5)
+            if on_scalar(i, w):
+                nc.scalar.activation(
+                    out=scaled[i, w][:], in_=fr[fo][:, :, wi, :], func=ACT.Copy, scale=rstd[i][:, w : w + 1]
+                )
+            else:
+                nc.vector.tensor_scalar_mul(scaled[i, w][:], fr[fo][:, :, wi, :], rstd[i][:, w : w + 1])
+
+        def rope(i, w):
             if w == 0:
                 t1[i] = work.tile([P, 2, D], F32, name="t1")
                 t2[i] = work.tile([P, 2, D], F32, name="t2")
-            nc.vector.scalar_tensor_tensor(
-                out=t1[i][:, w, :].rearrange("p (h m) -> p h m", h=HEADS),
-                in0=cos2[fo][:, wi : wi + 1, :].to_broadcast([P, HEADS, 2 * PAIRS]),
-                scalar=rstd[i][:, w : w + 1],
-                in1=u_bank[i, w][:],
-                op0=ALU.mult,
-                op1=ALU.mult,
+            table = scaled[i, w][:].rearrange("p s (j e) -> p e j s", e=2)
+            nc.vector.tensor_tensor(
+                out=t1[i][:, w, :].rearrange("p (h j e) -> p h j e", h=HEADS, e=2),
+                in0=u_bank[i, w][:].rearrange("p h (j e) -> p h j e", e=2),
+                in1=table[:, 0:1, :, 1:2].to_broadcast([P, HEADS, PAIRS, 2]),
+                op=ALU.mult,
             )
-
-        def rope_second(i, w):
-            t0, n = GROUPS[i]
-            fo, wi = divmod(t0 + w, 4)
-            nc.vector.scalar_tensor_tensor(
-                out=t2[i][:, w, :].rearrange("p (h m) -> p h m", h=HEADS),
-                in0=sin2[fo][:, wi : wi + 1, :].to_broadcast([P, HEADS, 2 * PAIRS]),
-                scalar=rstd[i][:, w : w + 1],
-                in1=u_bank[i, w][:].rearrange("p h (j e) -> p (h j) e", e=2)[:, :, ::-1],
-                op0=ALU.mult,
-                op1=ALU.mult,
+            nc.vector.tensor_tensor(
+                out=t2[i][:, w, :].rearrange("p (h j e) -> p h j e", h=HEADS, e=2),
+                in0=u_bank[i, w][:].rearrange("p h (j e) -> p h j e", e=2)[:, :, :, ::-1],
+                in1=table[:, 1:2, :, :].to_broadcast([P, HEADS, PAIRS, 2]),
+                op=ALU.mult,
             )
-
-        def rope(i, w):
-            rope_first(i, w)
-            rope_second(i, w)
 
         def add_and_store(engine, i, w0, m):
             t0 = GROUPS[i][0]
@@ -274,7 +260,7 @@ def tile_selfattention_pa_kernel(tc, x, freqs, w_words, w_scales, b, g, out):
             square_and_gain(0, c)
         copy_x(2, 0)
         quantize(2)
-        build_tables(0)
+        negate_freqs(0)
         copy_x(3, 0)
 
         for a in range(-1, n_groups):
@@ -303,9 +289,13 @@ def tile_selfattention_pa_kernel(tc, x, freqs, w_words, w_scales, b, g, out):
             if has_f:
                 transpose_x(f, 0)
             if has_mid:
-                root(mid)
+                inverse_root(mid)
             if has_nxt:
                 square(nxt, 2)
+            if has_mid:
+                for w in range(GROUPS[mid][1]):
+                    if on_scalar(mid, w):
+                        scale_freqs(mid, w)
             if has_nxt:
                 gain(nxt, 2)
                 square_and_gain(nxt, 3)
@@ -313,12 +303,14 @@ def tile_selfattention_pa_kernel(tc, x, freqs, w_words, w_scales, b, g, out):
                 rope(a, 1)
             if has_f and f < FIRST_SCALAR_COPY_GROUP:
                 copy_x(f, 0)
-            if has_mid:
-                invert(mid)
             if f - 1 < n_groups:
                 quantize(f - 1)
+            if has_mid:
+                for w in range(GROUPS[mid][1]):
+                    if not on_scalar(mid, w):
+                        scale_freqs(mid, w)
             if a in TABLE_STEPS:
-                build_tables(TABLE_STEPS[a])
+                negate_freqs(TABLE_STEPS[a])
             if 0 <= a < n_groups - 2:
                 add_and_store(nc.gpsimd, a, 0, n_a)
             if has_f and f >= FIRST_SCALAR_COPY_GROUP:

from contextlib import ExitStack

import concourse.mybir as mybir
from concourse.masks import make_identity

F32 = mybir.dt.float32
BF16 = mybir.dt.bfloat16
I32 = mybir.dt.int32
U32 = mybir.dt.uint32
U8 = mybir.dt.uint8
E5M2X4 = mybir.dt.float8_e5m2_x4
E2M1X4 = mybir.dt.float4_e2m1fn_x4
ACT = mybir.ActivationFunctionType
ALU = mybir.AluOpType

P = 128
S, D = 2560, 512
HEADS, PAIRS = 4, 64
EPS = 1e-5
FLOPS = 2 * S * D * D

SIZES = [1] + [2] * 9 + [1]
GROUPS = [(sum(SIZES[:i]), n) for i, n in enumerate(SIZES)]
FIRST_SCALAR_COPY_GROUP = 4
TABLE_STEPS = {-1: 1, 0: 2, 1: 3, 2: 4}
PLAIN = (4, 5)
SCALE_S = 6
SCALE_BOTH = 8


def tile_selfattention_pa_kernel(tc, x, freqs, w_words, w_scales, b, g, out):
    nc = tc.nc
    n_groups = len(GROUPS)
    x_rows = x[0].rearrange("(fo q wi) d -> fo q wi d", q=P, wi=4)
    out_rows = out[0].rearrange("(fo p wi) d -> fo p wi d", p=P, wi=4)
    freq_rows = freqs.rearrange(
        "(fo fi ho hi wo wi) o j e -> fo ho wo fi hi (wi o j e)", fi=8, ho=2, hi=4, wo=2, wi=4
    )

    with ExitStack() as ctx:
        keep = ctx.enter_context(tc.tile_pool(name="keep", bufs=1))
        work = ctx.enter_context(tc.tile_pool(name="work", bufs=3))
        psum = ctx.enter_context(tc.psum_pool(name="psum", bufs=2))
        ctx.enter_context(tc.manual_schedule())

        ident = keep.tile([P, P], F32, name="ident")
        perm = keep.tile([P, P], F32, name="perm")
        words = keep.tile([P, 2 * D], U8, name="words", align_bytes=64)
        plane = keep.tile([P, 4, D], U8, name="plane", align_bytes=64)
        bg_rows = keep.tile([8, P], BF16, name="bg_rows")
        bg_square = keep.tile([P, P], F32, name="bg_square")
        bg = keep.tile([P, 8], F32, name="bg")
        gb = keep.tile([P, HEADS], F32, name="gb")

        x_sb, grouped, codes, scales, fr = {}, {}, {}, {}, {}
        mm_pair, scaled = {}, {}
        xt_bank, mm_bank, ss_bank, u_bank = {}, {}, {}, {}
        u_sb, sq_sb, ssum, std, rstd, t1, t2 = {}, {}, {}, {}, {}, {}, {}

        def load_x(fo, w0, n):
            rows = keep.tile([P, n, D], BF16, name="x%d_%d" % (fo, w0))
            nc.sync.dma_start(out=rows[:], in_=x_rows[fo, :, w0 : w0 + n, :])
            for w in range(n):
                x_sb[4 * fo + w0 + w] = rows[:, w, :]

        def load_freqs(fo):
            fr[fo] = keep.tile([P, 2, 4, 2 * PAIRS], BF16, name="fr%d" % fo)
            flat = fr[fo][:, 1].rearrange("p w m -> p (w m)")
            for ho in range(2):
                for wo in range(2):
                    p0 = 64 * ho + 32 * wo
                    nc.sync.dma_start(out=flat[p0 : p0 + 32, :], in_=freq_rows[fo, ho, wo])

        def transpose_x(i, half):
            t0, n = GROUPS[i]
            bank = psum.tile([P, 2, 2, P], F32, name="xt_bank", tag="u", bufs=3)
            xt_bank[i, half] = bank
            for w in range(2 * half, min(n, 2 * half + 2)):
                x_words = x_sb[t0 + w].bitcast(F32)
                for u in range(2):
                    nc.tensor.transpose(bank[:, w - 2 * half, u, :], x_words[:, u : 256 : 2], perm[:])

        def copy_x(i, half):
            n = GROUPS[i][1]
            if half == 0:
                grouped[i] = keep.tile([P, n * D], BF16, name="grouped%d" % i, align_bytes=64)
            m = min(n - 2 * half, 2)
            dst = grouped[i][:, 2 * half * D : (2 * half + m) * D].bitcast(F32)
            dst = dst.rearrange("p (t r u) -> p t r u", r=P, u=2)
            src = xt_bank[i, half][:, 0:m, :, :].rearrange("p t u r -> p t r u")
            if i >= FIRST_SCALAR_COPY_GROUP:
                nc.scalar.copy(out=dst, in_=src)
            else:
                nc.vector.tensor_copy(out=dst, in_=src)

        def quantize(i):
            n = GROUPS[i][1]
            codes[i] = keep.tile([P, n * P], U32, name="codes%d" % i, align_bytes=64)
            scales[i] = keep.tile([P, n * P], U8, name="scales%d" % i, align_bytes=64)
            nc.vector.quantize_mx(out=codes[i][:].bitcast(E5M2X4), scales=scales[i][:], in_=grouped[i][:])

        def project(i, c):
            n = GROUPS[i][1]
            if c % 2 == 0:
                mm_pair[i, c // 2] = psum.tile([P, 2, 2 * P], F32, name="mm_bank", tag="mm", bufs=4)
            mm_bank[i, c] = mm_pair[i, c // 2][:, c % 2, :]
            nc.tensor.matmul_mx(
                out=mm_bank[i, c][:, : n * P],
                lhsT=words[:, 2 * P * c : 2 * P * (c + 1)].bitcast(E2M1X4),
                lhsT_scale=plane[:, 0, P * c : P * (c + 1)],
                rhs=codes[i][:].bitcast(E5M2X4),
                rhs_scale=scales[i][:],
                start=True,
                stop=True,
            )

        def square(i, c):
            n = GROUPS[i][1]
            if c == 0:
                u_sb[i] = work.tile([P, HEADS, D], F32, name="u_sb")
                sq_sb[i] = work.tile([P, HEADS, D], F32, name="sq_sb", bufs=2)
            src = mm_bank[i, c][:, : n * P]
            nc.scalar.activation(out=sq_sb[i][:, c, : n * P], in_=src, func=ACT.Square, bias=bg[:, c : c + 1])

        def gain(i, c):
            n = GROUPS[i][1]
            nc.scalar.activation(
                out=u_sb[i][:, c, : n * P],
                in_=mm_bank[i, c][:, : n * P],
                func=ACT.Identity,
                bias=gb[:, c : c + 1],
                scale=bg[:, HEADS + c : HEADS + c + 1],
            )

        def transpose_squares(i, c):
            n = GROUPS[i][1]
            if c == 0:
                ss_bank[i] = psum.tile([P, 4, P], F32, name="ss_bank", tag="ss", bufs=1)
            for w in range(n):
                nc.tensor.matmul(
                    out=ss_bank[i][:, w, :],
                    lhsT=sq_sb[i][:, c, w * P : (w + 1) * P],
                    rhs=ident[:],
                    is_transpose=(c * n + w not in PLAIN),
                    start=(c == 0 and w == 0),
                    stop=(c == HEADS - 1 and w == n - 1),
                )

        def sum_squares(i):
            n = GROUPS[i][1]
            ssum[i] = keep.tile([P, n], F32, name="ssum%d" % i)
            nc.vector.tensor_reduce(out=ssum[i][:], in_=ss_bank[i][:, :n, :], axis=mybir.AxisListType.X, op=ALU.add)

        def inverse_root(i):
            n = GROUPS[i][1]
            rstd[i] = keep.tile([P, n], F32, name="rstd%d" % i)
            nc.scalar.activation(out=rstd[i][:], in_=ssum[i][:], func=ACT.Abs_reciprocal_sqrt, scale=1.0 / D, bias=EPS)

        def transpose_u(i, w):
            bank = psum.tile([P, HEADS, P], F32, name="u_bank", tag="u", bufs=3)
            u_bank[i, w] = bank
            for c in range(HEADS):
                nc.tensor.transpose(bank[:, c, :], u_sb[i][:, c, w * P : (w + 1) * P], ident[:])

        def negate_freqs(fo):
            nc.vector.tensor_scalar_mul(fr[fo][:, 0], fr[fo][:, 1], -1.0)

        def on_scalar(i, w):
            return (w == 1 and i >= SCALE_S) or i >= SCALE_BOTH

        def scale_freqs(i, w):
            fo, wi = divmod(GROUPS[i][0] + w, 4)
            scaled[i, w] = work.tile([P, 2, 2 * PAIRS], F32, name="scaled", bufs=5)
            if on_scalar(i, w):
                nc.scalar.activation(
                    out=scaled[i, w][:], in_=fr[fo][:, :, wi, :], func=ACT.Copy, scale=rstd[i][:, w : w + 1]
                )
            else:
                nc.vector.tensor_scalar_mul(scaled[i, w][:], fr[fo][:, :, wi, :], rstd[i][:, w : w + 1])

        def rope(i, w):
            if w == 0:
                t1[i] = work.tile([P, 2, D], F32, name="t1")
                t2[i] = work.tile([P, 2, D], F32, name="t2")
            table = scaled[i, w][:].rearrange("p s (j e) -> p e j s", e=2)
            nc.vector.tensor_tensor(
                out=t1[i][:, w, :].rearrange("p (h j e) -> p h j e", h=HEADS, e=2),
                in0=u_bank[i, w][:].rearrange("p h (j e) -> p h j e", e=2),
                in1=table[:, 0:1, :, 1:2].to_broadcast([P, HEADS, PAIRS, 2]),
                op=ALU.mult,
            )
            nc.vector.tensor_tensor(
                out=t2[i][:, w, :].rearrange("p (h j e) -> p h j e", h=HEADS, e=2),
                in0=u_bank[i, w][:].rearrange("p h (j e) -> p h j e", e=2)[:, :, :, ::-1],
                in1=table[:, 1:2, :, :].to_broadcast([P, HEADS, PAIRS, 2]),
                op=ALU.mult,
            )

        def add_and_store(engine, i, w0, m):
            t0 = GROUPS[i][0]
            res = work.tile([P, 2, D], F32, name="res", bufs=4)
            engine.tensor_tensor(
                out=res[:, :m, :],
                in0=t1[i][:, w0 : w0 + m, :],
                in1=t2[i][:, w0 : w0 + m, :],
                op=ALU.add,
            )
            for w in range(m):
                fo, wi = divmod(t0 + w0 + w, 4)
                nc.sync.dma_start(out=out_rows[fo, :, wi, :], in_=res[:, w, :])

        make_identity(nc, ident[:])
        load_x(0, 0, 1)
        nc.scalar.dma_start(out=bg_rows[0:4, :], in_=b.rearrange("(c m) -> c m", m=P))
        nc.scalar.dma_start(out=bg_rows[4:8, :], in_=g.rearrange("(c m) -> c m", m=P))
        nc.sync.dma_start(
            out=plane[0:4, :, :].bitcast(I32), in_=w_scales[0].rearrange("(q r) n -> r q n", r=4).bitcast(I32)
        )
        nc.sync.dma_start(out=words[:].bitcast(I32), in_=w_words[0].bitcast(I32))
        load_x(0, 1, 3)
        load_x(1, 0, 4)
        load_freqs(0)
        for fo in range(2, 5):
            load_x(fo, 0, 4)
            load_freqs(fo - 1)
        load_freqs(4)
        nc.vector.memset(bg_square[:], 0.0)
        ident_split = ident[:].rearrange("r (fi ho hi wo) -> r ho wo fi hi", fi=8, ho=2, hi=4)
        perm_split = perm[:].rearrange("r (ho wo fi hi) -> r ho wo fi hi", ho=2, wo=2, fi=8)
        for ho in range(2):
            nc.vector.tensor_copy(out=perm_split[:, ho], in_=ident_split[:, ho])
        nc.vector.tensor_copy(out=bg_square[0:8, :], in_=bg_rows[:])
        for q in range(1, 4):
            nc.vector.tensor_copy(out=plane[32 * q : 32 * q + 4, 0, :].bitcast(I32), in_=plane[0:4, q, :].bitcast(I32))

        transpose_x(0, 0)
        bg_bank = psum.tile([P, 4, P], F32, name="bg_bank", tag="ss", bufs=1)
        nc.tensor.transpose(bg_bank[:, 0, :], bg_square[:], ident[:])
        copy_x(0, 0)
        nc.vector.tensor_copy(out=bg[:], in_=bg_bank[:, 0, 0:8])
        quantize(0)
        nc.vector.tensor_tensor(out=gb[:], in0=bg[:, 0:HEADS], in1=bg[:, HEADS:8], op=ALU.mult)

        def project_all(i):
            for c in range(HEADS):
                project(i, c)

        def square_and_gain(i, c):
            square(i, c)
            gain(i, c)

        transpose_x(1, 0)
        project_all(0)
        copy_x(1, 0)
        transpose_x(2, 0)
        quantize(1)
        project_all(1)
        transpose_x(3, 0)
        for c in range(HEADS):
            square_and_gain(0, c)
        copy_x(2, 0)
        quantize(2)
        negate_freqs(0)
        copy_x(3, 0)

        for a in range(-1, n_groups):
            mid, nxt, far, f = a + 1, a + 2, a + 3, a + 5
            n_a = GROUPS[a][1] if a >= 0 else 0
            has_mid = mid < n_groups
            has_nxt = nxt < n_groups
            has_f = f < n_groups
            if has_mid:
                for c in range(HEADS):
                    transpose_squares(mid, c)
            if n_a > 1:
                transpose_u(a, 1)
            if n_a > 0:
                rope(a, 0)
            if a == n_groups - 2:
                add_and_store(nc.gpsimd, a, 0, 1)
            if has_mid:
                sum_squares(mid)
                transpose_u(mid, 0)
            if has_nxt:
                square_and_gain(nxt, 0)
                square_and_gain(nxt, 1)
            if far < n_groups:
                project_all(far)
            if has_f:
                transpose_x(f, 0)
            if has_mid:
                inverse_root(mid)
            if has_nxt:
                square(nxt, 2)
            if has_mid:
                for w in range(GROUPS[mid][1]):
                    if on_scalar(mid, w):
                        scale_freqs(mid, w)
            if has_nxt:
                gain(nxt, 2)
                square_and_gain(nxt, 3)
            if n_a > 1:
                rope(a, 1)
            if has_f and f < FIRST_SCALAR_COPY_GROUP:
                copy_x(f, 0)
            if f - 1 < n_groups:
                quantize(f - 1)
            if has_mid:
                for w in range(GROUPS[mid][1]):
                    if not on_scalar(mid, w):
                        scale_freqs(mid, w)
            if a in TABLE_STEPS:
                negate_freqs(TABLE_STEPS[a])
            if 0 <= a < n_groups - 2:
                add_and_store(nc.gpsimd, a, 0, n_a)
            if has_f and f >= FIRST_SCALAR_COPY_GROUP:
                copy_x(f, 0)

        add_and_store(nc.vector, n_groups - 2, 1, 1)
        add_and_store(nc.vector, n_groups - 1, 0, 1)
